import numpy as np
import ml_dtypes


def mxq(x, axis, fmt="e4m3"):
    dtype, down = {"e4m3": (ml_dtypes.float8_e4m3fn, 7), "e5m2": (ml_dtypes.float8_e5m2, 14)}[fmt]
    v = np.moveaxis(np.asarray(x, np.float32).astype(ml_dtypes.bfloat16).astype(np.float64), axis, -1)
    blocks = v.reshape(v.shape[:-1] + (-1, 32))
    amax = np.abs(blocks).max(-1, keepdims=True)
    byte = np.maximum(np.where(amax > 0, np.frexp(amax)[1] - 1 + 127, 0) - down, 1)
    scale = np.exp2(byte - 127.0)
    codes = (blocks / scale).astype(np.float32).astype(dtype).astype(np.float64)
    return np.moveaxis((codes * scale).reshape(v.shape), -1, axis)


WIDE = False


def mx_kscale(k):
    if not WIDE:
        return np.ones(k)
    levels = np.array([10, -10, 5, -5, 0])
    a = np.random.permutation(np.resize(levels, k // 512 * 4)).reshape(k // 512, 4)
    idx = np.arange(k)
    return np.exp2(a[idx // 512, idx % 128 // 32])


BF16 = ml_dtypes.bfloat16


def bf(x):
    return np.asarray(x, np.float32).astype(BF16)


def f64(x):
    return np.asarray(x).astype(np.float64)


B, S, H = 8, 49, 512
N = B * (S - 1)
G = 0.75


def setup_inputs():
    s = mx_kscale(H)
    return {"x": bf(np.random.standard_normal((B, S, H)) * s),
            "k1": bf(np.random.standard_normal((N, H)) * G * s),
            "k2": bf(np.random.standard_normal((N, H)) * G * np.sqrt(1.0 + 0.25 * G * G) * s),
            "coefficients": bf(np.random.standard_normal((H, H)) * G / np.sqrt(H) * s[:, None] / s[None, :])}


def reference(x, k1, k2, coefficients):
    x, k1, k2 = f64(x), f64(k1), f64(k2)
    y = x[:, :-1, :].reshape(-1, H)
    cq = mxq(f64(coefficients), 1, "e4m3")
    k3 = mxq(y + 0.5 * k2, 1, "e4m3") @ cq.T
    k4 = mxq(y + k3, 1, "e4m3") @ cq.T
    y1 = y + (k1 + 2.0 * k2 + 2.0 * k3 + k4) / 6.0
    return y1.reshape(B, S - 1, H) - x[:, 1:, :]

@@ -1,0 +1,185 @@
+from contextlib import ExitStack
+
+import concourse.mybir as mybir
+from concourse.masks import make_identity
+
+F32 = mybir.dt.float32
+BF16 = mybir.dt.bfloat16
+U32 = mybir.dt.uint32
+U8 = mybir.dt.uint8
+FP8X4 = mybir.dt.float8_e4m3fn_x4
+ALU = mybir.AluOpType
+COPY = mybir.ActivationFunctionType.Copy
+
+P = 128
+B = 8
+S = 49
+H = 512
+R = 3
+Q = (S - 1) // R
+PACK = 4
+HALF = 2
+WORDS = H // HALF
+
+FLOPS = 2 * 2 * B * (S - 1) * H * H
+
+
+def tile_sindylossmixin_pa_s_kernel(tc, x, k1, k2, coefficients, out):
+    nc = tc.nc
+    with ExitStack() as ctx:
+        keep = ctx.enter_context(tc.tile_pool(name="keep", bufs=1))
+        psum = ctx.enter_context(tc.psum_pool(name="psum", bufs=1))
+
+        x_sb = keep.tile([P, R + 1, H], BF16)
+        k1_sb = keep.tile([P, R, H], BF16)
+        k2_sb = keep.tile([P, R, H], BF16)
+        c_sb = keep.tile([P, HALF, HALF, H], BF16)
+        nc.sync.dma_start(
+            out=x_sb[:, 0:R, :].rearrange("p r h -> p (r h)"),
+            in_=x[:, 0 : S - 1, :].rearrange("b (q r) h -> q b (r h)", r=R),
+        )
+        nc.sync.dma_start(
+            out=x_sb[:, R, :],
+            in_=x[:, 1:S, :].rearrange("b (q r) h -> q b r h", r=R)[:, :, R - 1, :],
+        )
+        nc.sync.dma_start(
+            out=k2_sb[:].rearrange("p r h -> p (r h)"),
+            in_=k2.rearrange("(b q r) h -> q b (r h)", b=B, q=Q, r=R),
+        )
+        c_rows = coefficients.rearrange("(u m e) j -> u m (e j)", u=HALF, e=HALF)
+        for u in range(HALF):
+            nc.sync.dma_start(out=c_sb[:, u, :, :].rearrange("m e j -> m (e j)"), in_=c_rows[u])
+        nc.sync.dma_start(
+            out=k1_sb[:].rearrange("p r h -> p (r h)"),
+            in_=k1.rearrange("(b q r) h -> q b (r h)", b=B, q=Q, r=R),
+        )
+
+        ident = keep.tile([P, P], F32)
+        make_identity(nc, ident[:])
+
+        warm = keep.tile([P, 2], F32)
+        nc.vector.memset(warm[:, 0:1], 0.0)
+        nc.scalar.activation(out=warm[:, 1:2], in_=warm[:, 0:1], func=COPY)
+
+        def transpose_words(bank, words):
+            for u in range(HALF):
+                nc.tensor.transpose(bank[:, u, :], words[:, u * P : (u + 1) * P], ident[:])
+
+        x_words = x_sb[:].bitcast(F32)
+        k2_words = k2_sb[:].bitcast(F32)
+        c_words = c_sb[:].bitcast(F32)
+        yT = keep.tile([P, R, P, PACK], BF16, align_bytes=64)
+        half_k2T = keep.tile([P, R, P, PACK], BF16, align_bytes=64)
+        aT = keep.tile([P, R, P, PACK], BF16, align_bytes=64)
+        zT = keep.tile([P, R, P, PACK], BF16, align_bytes=64)
+        cT = keep.tile([P, H, PACK], BF16, align_bytes=64)
+        a_codes = keep.tile([P, R * P], U32, align_bytes=64)
+        a_scales = keep.tile([P, R * P], U8, align_bytes=64)
+        z_codes = keep.tile([P, R * P], U32, align_bytes=64)
+        z_scales = keep.tile([P, R * P], U8, align_bytes=64)
+        c_codes = keep.tile([P, H], U32, align_bytes=64)
+        c_scales = keep.tile([P, H], U8, align_bytes=64)
+
+        for r in range(R):
+            yT_ps = psum.tile([P, HALF, P], F32, tag="y_then_k3", bufs=R)
+            transpose_words(yT_ps, x_words[:, r, :])
+            nc.scalar.copy(
+                out=yT[:, r, :, :].bitcast(F32), in_=yT_ps[:].rearrange("p u n -> p n u")
+            )
+        for r in range(R):
+            k2T_ps = psum.tile([P, HALF, P], F32, tag="k2_then_sum", bufs=R)
+            transpose_words(k2T_ps, k2_words[:, r, :])
+            nc.scalar.activation(
+                out=half_k2T[:, r, :, :].rearrange("p n (u e) -> p n u e", e=HALF),
+                in_=k2T_ps[:].bitcast(BF16).rearrange("p u (n e) -> p n u e", e=HALF),
+                func=COPY,
+                scale=0.5,
+            )
+            nc.vector.tensor_tensor(
+                out=aT[:, r, :, :], in0=yT[:, r, :, :], in1=half_k2T[:, r, :, :], op=ALU.add
+            )
+            cols = slice(r * P, (r + 1) * P)
+            nc.vector.quantize_mx(
+                out=a_codes[:, cols].bitcast(FP8X4),
+                scales=a_scales[:, cols],
+                in_=aT[:, r, :, :].rearrange("p n t -> p (n t)"),
+            )
+
+        for ui in range(HALF):
+            cT_ps = psum.tile([P, HALF, HALF, P], F32, tag="c", bufs=HALF)
+            for ei in range(HALF):
+                transpose_words(cT_ps[:, ei, :, :], c_words[:, ui, ei, :])
+            cols = slice(ui * HALF * P, (ui + 1) * HALF * P)
+            nc.scalar.copy(
+                out=cT[:, cols, :].bitcast(F32).rearrange("p (e m) u -> p e m u", e=HALF),
+                in_=cT_ps[:].rearrange("p e u m -> p e m u"),
+            )
+            nc.vector.quantize_mx(
+                out=c_codes[:, cols].bitcast(FP8X4),
+                scales=c_scales[:, cols],
+                in_=cT[:, cols, :].rearrange("p i t -> p (i t)"),
+            )
+
+        diff = keep.tile([P, R, H], F32)
+        nc.vector.tensor_tensor(
+            out=diff[:], in0=x_sb[:, 0:R, :], in1=x_sb[:, 1 : R + 1, :], op=ALU.subtract
+        )
+        k_sum = keep.tile([P, R, H], F32)
+        nc.vector.scalar_tensor_tensor(
+            out=k_sum[:], in0=k2_sb[:], scalar=2.0, in1=k1_sb[:], op0=ALU.mult, op1=ALU.add
+        )
+        base = keep.tile([P, R, H], F32)
+        nc.vector.scalar_tensor_tensor(
+            out=base[:], in0=k_sum[:], scalar=1.0 / 6.0, in1=diff[:], op0=ALU.mult, op1=ALU.add
+        )
+
+        out_rows = out.rearrange("b (q r) h -> q b r h", r=R)
+        result = keep.tile([P, R, H], F32)
+        for r in range(R):
+            cols = slice(r * P, (r + 1) * P)
+            k3T_ps = psum.tile([P, PACK, P], F32, tag="y_then_k3", bufs=R)
+            for t in range(PACK):
+                i_cols = slice(t * P, (t + 1) * P)
+                nc.tensor.matmul_mx(
+                    out=k3T_ps[:, t, :],
+                    lhsT=c_codes[:, i_cols].bitcast(FP8X4),
+                    lhsT_scale=c_scales[:, i_cols],
+                    rhs=a_codes[:, cols].bitcast(FP8X4),
+                    rhs_scale=a_scales[:, cols],
+                    start=True,
+                    stop=True,
+                )
+            nc.vector.tensor_tensor(
+                out=zT[:, r, :, :],
+                in0=k3T_ps[:].rearrange("p t n -> p n t"),
+                in1=yT[:, r, :, :],
+                op=ALU.add,
+            )
+            nc.vector.quantize_mx(
+                out=z_codes[:, cols].bitcast(FP8X4),
+                scales=z_scales[:, cols],
+                in_=zT[:, r, :, :].rearrange("p n t -> p (n t)"),
+            )
+            sum_ps = psum.tile([P, HALF, HALF, P], F32, tag="k2_then_sum", bufs=R)
+            passes = [(a_codes, a_scales), (a_codes, a_scales), (z_codes, z_scales)]
+            for n_pass, (codes, scales) in enumerate(passes):
+                nc.tensor.matmul_mx(
+                    out=sum_ps[:].rearrange("p u e m -> p (u e m)"),
+                    lhsT=codes[:, cols].bitcast(FP8X4),
+                    lhsT_scale=scales[:, cols],
+                    rhs=c_codes[:].bitcast(FP8X4),
+                    rhs_scale=c_scales[:],
+                    start=(n_pass == 0),
+                    stop=(n_pass == len(passes) - 1),
+                )
+            for u in range(HALF):
+                i_cols = slice(u * HALF * P, (u + 1) * HALF * P)
+                nc.vector.scalar_tensor_tensor(
+                    out=result[:, r, i_cols].rearrange("p (m e) -> p m e", e=HALF),
+                    in0=sum_ps[:, u, :, :].rearrange("p e m -> p m e"),
+                    scalar=1.0 / 6.0,
+                    in1=base[:, r, i_cols].rearrange("p (m e) -> p m e", e=HALF),
+                    op0=ALU.mult,
+                    op1=ALU.add,
+                )
+            nc.sync.dma_start(out=out_rows[:, :, r, :], in_=result[:, r, :])

@@ -19,7 +19,6 @@ R = 3
 Q = (S - 1) // R
 PACK = 4
 HALF = 2
-WORDS = H // HALF
 
 FLOPS = 2 * 2 * B * (S - 1) * H * H
 
@@ -29,6 +28,7 @@ def tile_sindylossmixin_pa_s_kernel(tc, x, k1, k2, coefficients, out):
     with ExitStack() as ctx:
         keep = ctx.enter_context(tc.tile_pool(name="keep", bufs=1))
         psum = ctx.enter_context(tc.psum_pool(name="psum", bufs=1))
+        ctx.enter_context(tc.manual_schedule())
 
         x_sb = keep.tile([P, R + 1, H], BF16)
         k1_sb = keep.tile([P, R, H], BF16)
@@ -46,13 +46,13 @@ def tile_sindylossmixin_pa_s_kernel(tc, x, k1, k2, coefficients, out):
             out=k2_sb[:].rearrange("p r h -> p (r h)"),
             in_=k2.rearrange("(b q r) h -> q b (r h)", b=B, q=Q, r=R),
         )
-        c_rows = coefficients.rearrange("(u m e) j -> u m (e j)", u=HALF, e=HALF)
-        for u in range(HALF):
-            nc.sync.dma_start(out=c_sb[:, u, :, :].rearrange("m e j -> m (e j)"), in_=c_rows[u])
         nc.sync.dma_start(
             out=k1_sb[:].rearrange("p r h -> p (r h)"),
             in_=k1.rearrange("(b q r) h -> q b (r h)", b=B, q=Q, r=R),
         )
+        c_rows = coefficients.rearrange("(u m e) j -> e m u j", u=HALF, e=HALF)
+        for e in range(HALF):
+            nc.sync.dma_start(out=c_sb[:, e, :, :], in_=c_rows[e])
 
         ident = keep.tile([P, P], F32)
         make_identity(nc, ident[:])
@@ -79,6 +79,18 @@ def tile_sindylossmixin_pa_s_kernel(tc, x, k1, k2, coefficients, out):
         z_scales = keep.tile([P, R * P], U8, align_bytes=64)
         c_codes = keep.tile([P, H], U32, align_bytes=64)
         c_scales = keep.tile([P, H], U8, align_bytes=64)
+        diff = keep.tile([P, R, H], F32)
+        k_sum = keep.tile([P, R, H], F32)
+        base = keep.tile([P, R, H], F32)
+        result = keep.tile([P, R, H], F32)
+
+        def quantise(codes, scales, cols, grouped):
+            nc.vector.quantize_mx(
+                out=codes[:, cols].bitcast(FP8X4), scales=scales[:, cols], in_=grouped
+            )
+
+        def chunk(r):
+            return slice(r * P, (r + 1) * P)
 
         for r in range(R):
             yT_ps = psum.tile([P, HALF, P], F32, tag="y_then_k3", bufs=R)
@@ -86,6 +98,10 @@ def tile_sindylossmixin_pa_s_kernel(tc, x, k1, k2, coefficients, out):
             nc.scalar.copy(
                 out=yT[:, r, :, :].bitcast(F32), in_=yT_ps[:].rearrange("p u n -> p n u")
             )
+        nc.vector.tensor_tensor(
+            out=diff[:], in0=x_sb[:, 0:R, :], in1=x_sb[:, 1 : R + 1, :], op=ALU.subtract
+        )
+
         for r in range(R):
             k2T_ps = psum.tile([P, HALF, P], F32, tag="k2_then_sum", bufs=R)
             transpose_words(k2T_ps, k2_words[:, r, :])
@@ -95,91 +111,77 @@ def tile_sindylossmixin_pa_s_kernel(tc, x, k1, k2, coefficients, out):
                 func=COPY,
                 scale=0.5,
             )
-            nc.vector.tensor_tensor(
-                out=aT[:, r, :, :], in0=yT[:, r, :, :], in1=half_k2T[:, r, :, :], op=ALU.add
-            )
-            cols = slice(r * P, (r + 1) * P)
-            nc.vector.quantize_mx(
-                out=a_codes[:, cols].bitcast(FP8X4),
-                scales=a_scales[:, cols],
-                in_=aT[:, r, :, :].rearrange("p n t -> p (n t)"),
-            )
-
-        for ui in range(HALF):
-            cT_ps = psum.tile([P, HALF, HALF, P], F32, tag="c", bufs=HALF)
-            for ei in range(HALF):
-                transpose_words(cT_ps[:, ei, :, :], c_words[:, ui, ei, :])
-            cols = slice(ui * HALF * P, (ui + 1) * HALF * P)
-            nc.scalar.copy(
-                out=cT[:, cols, :].bitcast(F32).rearrange("p (e m) u -> p e m u", e=HALF),
-                in_=cT_ps[:].rearrange("p e u m -> p e m u"),
-            )
-            nc.vector.quantize_mx(
-                out=c_codes[:, cols].bitcast(FP8X4),
-                scales=c_scales[:, cols],
-                in_=cT[:, cols, :].rearrange("p i t -> p (i t)"),
-            )
-
-        diff = keep.tile([P, R, H], F32)
-        nc.vector.tensor_tensor(
-            out=diff[:], in0=x_sb[:, 0:R, :], in1=x_sb[:, 1 : R + 1, :], op=ALU.subtract
-        )
-        k_sum = keep.tile([P, R, H], F32)
         nc.vector.scalar_tensor_tensor(
             out=k_sum[:], in0=k2_sb[:], scalar=2.0, in1=k1_sb[:], op0=ALU.mult, op1=ALU.add
         )
-        base = keep.tile([P, R, H], F32)
+        nc.vector.tensor_tensor(out=aT[:], in0=yT[:], in1=half_k2T[:], op=ALU.add)
+
+        for e in range(HALF):
+            cT_ps = psum.tile([P, HALF, HALF, P], F32, tag="c", bufs=HALF)
+            for u in range(HALF):
+                transpose_words(cT_ps[:, u, :, :], c_words[:, e, u, :])
+            cols = slice(e * HALF * P, (e + 1) * HALF * P)
+            nc.scalar.copy(
+                out=cT[:, cols, :].bitcast(F32).rearrange("p (u m) w -> p u m w", u=HALF),
+                in_=cT_ps[:].rearrange("p u w m -> p u m w"),
+            )
+        half_cols = [slice(e * HALF * P, (e + 1) * HALF * P) for e in range(HALF)]
+        quantise(c_codes, c_scales, half_cols[0], cT[:, half_cols[0], :].rearrange("p i t -> p (i t)"))
+        for r in range(R):
+            quantise(a_codes, a_scales, chunk(r), aT[:, r, :, :].rearrange("p n t -> p (n t)"))
+        quantise(c_codes, c_scales, half_cols[1], cT[:, half_cols[1], :].rearrange("p i t -> p (i t)"))
         nc.vector.scalar_tensor_tensor(
             out=base[:], in0=k_sum[:], scalar=1.0 / 6.0, in1=diff[:], op0=ALU.mult, op1=ALU.add
         )
 
-        out_rows = out.rearrange("b (q r) h -> q b r h", r=R)
-        result = keep.tile([P, R, H], F32)
+        k3T_banks = []
         for r in range(R):
-            cols = slice(r * P, (r + 1) * P)
             k3T_ps = psum.tile([P, PACK, P], F32, tag="y_then_k3", bufs=R)
-            for t in range(PACK):
-                i_cols = slice(t * P, (t + 1) * P)
+            k3T_banks.append(k3T_ps)
+            for g in range(PACK):
                 nc.tensor.matmul_mx(
-                    out=k3T_ps[:, t, :],
-                    lhsT=c_codes[:, i_cols].bitcast(FP8X4),
-                    lhsT_scale=c_scales[:, i_cols],
-                    rhs=a_codes[:, cols].bitcast(FP8X4),
-                    rhs_scale=a_scales[:, cols],
+                    out=k3T_ps[:, g, :],
+                    lhsT=c_codes[:, chunk(g)].bitcast(FP8X4),
+                    lhsT_scale=c_scales[:, chunk(g)],
+                    rhs=a_codes[:, chunk(r)].bitcast(FP8X4),
+                    rhs_scale=a_scales[:, chunk(r)],
                     start=True,
                     stop=True,
                 )
-            nc.vector.tensor_tensor(
-                out=zT[:, r, :, :],
-                in0=k3T_ps[:].rearrange("p t n -> p n t"),
-                in1=yT[:, r, :, :],
-                op=ALU.add,
-            )
-            nc.vector.quantize_mx(
-                out=z_codes[:, cols].bitcast(FP8X4),
-                scales=z_scales[:, cols],
-                in_=zT[:, r, :, :].rearrange("p n t -> p (n t)"),
-            )
-            sum_ps = psum.tile([P, HALF, HALF, P], F32, tag="k2_then_sum", bufs=R)
+
+        for r in range(R + 1):
+            if r < R:
+                nc.vector.tensor_tensor(
+                    out=zT[:, r, :, :].rearrange("p n (u e) -> p n u e", e=HALF),
+                    in0=k3T_banks[r][:].rearrange("p (e u) n -> p n u e", e=HALF),
+                    in1=yT[:, r, :, :].rearrange("p n (u e) -> p n u e", e=HALF),
+                    op=ALU.add,
+                )
+            if r > 0:
+                quantise(
+                    z_codes, z_scales, chunk(r - 1), zT[:, r - 1, :, :].rearrange("p n t -> p (n t)")
+                )
+
+        out_rows = out.rearrange("b (q r) h -> q b r h", r=R)
+        for r in range(R):
+            sum_ps = psum.tile([P, H], F32, tag="k2_then_sum", bufs=R)
             passes = [(a_codes, a_scales), (a_codes, a_scales), (z_codes, z_scales)]
             for n_pass, (codes, scales) in enumerate(passes):
                 nc.tensor.matmul_mx(
-                    out=sum_ps[:].rearrange("p u e m -> p (u e m)"),
-                    lhsT=codes[:, cols].bitcast(FP8X4),
-                    lhsT_scale=scales[:, cols],
+                    out=sum_ps[:],
+                    lhsT=codes[:, chunk(r)].bitcast(FP8X4),
+                    lhsT_scale=scales[:, chunk(r)],
                     rhs=c_codes[:].bitcast(FP8X4),
                     rhs_scale=c_scales[:],
                     start=(n_pass == 0),
                     stop=(n_pass == len(passes) - 1),
                 )
-            for u in range(HALF):
-                i_cols = slice(u * HALF * P, (u + 1) * HALF * P)
-                nc.vector.scalar_tensor_tensor(
-                    out=result[:, r, i_cols].rearrange("p (m e) -> p m e", e=HALF),
-                    in0=sum_ps[:, u, :, :].rearrange("p e m -> p m e"),
-                    scalar=1.0 / 6.0,
-                    in1=base[:, r, i_cols].rearrange("p (m e) -> p m e", e=HALF),
-                    op0=ALU.mult,
-                    op1=ALU.add,
-                )
+            nc.vector.scalar_tensor_tensor(
+                out=result[:, r, :].rearrange("p (c e) -> p c e", e=HALF),
+                in0=sum_ps[:].rearrange("p (e c) -> p c e", e=HALF),
+                scalar=1.0 / 6.0,
+                in1=base[:, r, :].rearrange("p (c e) -> p c e", e=HALF),
+                op0=ALU.mult,
+                op1=ALU.add,
+            )
             nc.sync.dma_start(out=out_rows[:, :, r, :], in_=result[:, r, :])

@@ -81,6 +81,7 @@ def tile_sindylossmixin_pa_s_kernel(tc, x, k1, k2, coefficients, out):
         c_scales = keep.tile([P, H], U8, align_bytes=64)
         diff = keep.tile([P, R, H], F32)
         k_sum = keep.tile([P, R, H], F32)
+        k_sixth = keep.tile([P, R, H], F32)
         base = keep.tile([P, R, H], F32)
         result = keep.tile([P, R, H], F32)
 
@@ -127,12 +128,15 @@ def tile_sindylossmixin_pa_s_kernel(tc, x, k1, k2, coefficients, out):
             )
         half_cols = [slice(e * HALF * P, (e + 1) * HALF * P) for e in range(HALF)]
         quantise(c_codes, c_scales, half_cols[0], cT[:, half_cols[0], :].rearrange("p i t -> p (i t)"))
-        for r in range(R):
-            quantise(a_codes, a_scales, chunk(r), aT[:, r, :, :].rearrange("p n t -> p (n t)"))
+        quantise(a_codes, a_scales, chunk(0), aT[:, 0, :, :].rearrange("p n t -> p (n t)"))
         quantise(c_codes, c_scales, half_cols[1], cT[:, half_cols[1], :].rearrange("p i t -> p (i t)"))
-        nc.vector.scalar_tensor_tensor(
-            out=base[:], in0=k_sum[:], scalar=1.0 / 6.0, in1=diff[:], op0=ALU.mult, op1=ALU.add
-        )
+        for r in range(1, R):
+            quantise(a_codes, a_scales, chunk(r), aT[:, r, :, :].rearrange("p n t -> p (n t)"))
+        for r in range(R):
+            nc.scalar.activation(out=k_sixth[:, r, :], in_=k_sum[:, r, :], func=COPY, scale=1.0 / 6.0)
+            nc.gpsimd.tensor_tensor(
+                out=base[:, r, :], in0=k_sixth[:, r, :], in1=diff[:, r, :], op=ALU.add
+            )
 
         k3T_banks = []
         for r in range(R):

@@ -81,7 +81,6 @@ def tile_sindylossmixin_pa_s_kernel(tc, x, k1, k2, coefficients, out):
         c_scales = keep.tile([P, H], U8, align_bytes=64)
         diff = keep.tile([P, R, H], F32)
         k_sum = keep.tile([P, R, H], F32)
-        k_sixth = keep.tile([P, R, H], F32)
         base = keep.tile([P, R, H], F32)
         result = keep.tile([P, R, H], F32)
 
@@ -92,6 +91,16 @@ def tile_sindylossmixin_pa_s_kernel(tc, x, k1, k2, coefficients, out):
 
         def chunk(r):
             return slice(r * P, (r + 1) * P)
+
+        def add_k_sum(rows):
+            nc.vector.scalar_tensor_tensor(
+                out=k_sum[:, rows, :],
+                in0=k2_sb[:, rows, :],
+                scalar=2.0,
+                in1=k1_sb[:, rows, :],
+                op0=ALU.mult,
+                op1=ALU.add,
+            )
 
         for r in range(R):
             yT_ps = psum.tile([P, HALF, P], F32, tag="y_then_k3", bufs=R)
@@ -112,9 +121,7 @@ def tile_sindylossmixin_pa_s_kernel(tc, x, k1, k2, coefficients, out):
                 func=COPY,
                 scale=0.5,
             )
-        nc.vector.scalar_tensor_tensor(
-            out=k_sum[:], in0=k2_sb[:], scalar=2.0, in1=k1_sb[:], op0=ALU.mult, op1=ALU.add
-        )
+        add_k_sum(slice(0, R - 1))
         nc.vector.tensor_tensor(out=aT[:], in0=yT[:], in1=half_k2T[:], op=ALU.add)
 
         for e in range(HALF):
@@ -132,11 +139,10 @@ def tile_sindylossmixin_pa_s_kernel(tc, x, k1, k2, coefficients, out):
         quantise(c_codes, c_scales, half_cols[1], cT[:, half_cols[1], :].rearrange("p i t -> p (i t)"))
         for r in range(1, R):
             quantise(a_codes, a_scales, chunk(r), aT[:, r, :, :].rearrange("p n t -> p (n t)"))
-        for r in range(R):
-            nc.scalar.activation(out=k_sixth[:, r, :], in_=k_sum[:, r, :], func=COPY, scale=1.0 / 6.0)
-            nc.gpsimd.tensor_tensor(
-                out=base[:, r, :], in0=k_sixth[:, r, :], in1=diff[:, r, :], op=ALU.add
-            )
+        add_k_sum(slice(R - 1, R))
+        nc.vector.scalar_tensor_tensor(
+            out=base[:], in0=k_sum[:], scalar=1.0 / 6.0, in1=diff[:], op0=ALU.mult, op1=ALU.add
+        )
 
         k3T_banks = []
         for r in range(R):
@@ -153,6 +159,24 @@ def tile_sindylossmixin_pa_s_kernel(tc, x, k1, k2, coefficients, out):
                     stop=True,
                 )
 
+        def row_pass(bank, codes, scales, r, start, stop):
+            nc.tensor.matmul_mx(
+                out=bank[:],
+                lhsT=codes[:, chunk(r)].bitcast(FP8X4),
+                lhsT_scale=scales[:, chunk(r)],
+                rhs=c_codes[:].bitcast(FP8X4),
+                rhs_scale=c_scales[:],
+                start=start,
+                stop=stop,
+            )
+
+        sum_banks = []
+        for r in range(R):
+            sum_ps = psum.tile([P, H], F32, tag="k2_then_sum", bufs=R)
+            sum_banks.append(sum_ps)
+            row_pass(sum_ps, a_codes, a_scales, r, True, False)
+            row_pass(sum_ps, a_codes, a_scales, r, False, False)
+
         for r in range(R + 1):
             if r < R:
                 nc.vector.tensor_tensor(
@@ -168,18 +192,8 @@ def tile_sindylossmixin_pa_s_kernel(tc, x, k1, k2, coefficients, out):
 
         out_rows = out.rearrange("b (q r) h -> q b r h", r=R)
         for r in range(R):
-            sum_ps = psum.tile([P, H], F32, tag="k2_then_sum", bufs=R)
-            passes = [(a_codes, a_scales), (a_codes, a_scales), (z_codes, z_scales)]
-            for n_pass, (codes, scales) in enumerate(passes):
-                nc.tensor.matmul_mx(
-                    out=sum_ps[:],
-                    lhsT=codes[:, chunk(r)].bitcast(FP8X4),
-                    lhsT_scale=scales[:, chunk(r)],
-                    rhs=c_codes[:].bitcast(FP8X4),
-                    rhs_scale=c_scales[:],
-                    start=(n_pass == 0),
-                    stop=(n_pass == len(passes) - 1),
-                )
+            sum_ps = sum_banks[r]
+            row_pass(sum_ps, z_codes, z_scales, r, False, True)
             nc.vector.scalar_tensor_tensor(
                 out=result[:, r, :].rearrange("p (c e) -> p c e", e=HALF),
                 in0=sum_ps[:].rearrange("p (e c) -> p c e", e=HALF),

from contextlib import ExitStack

import concourse.mybir as mybir
from concourse.masks import make_identity

F32 = mybir.dt.float32
BF16 = mybir.dt.bfloat16
U32 = mybir.dt.uint32
U8 = mybir.dt.uint8
FP8X4 = mybir.dt.float8_e4m3fn_x4
ALU = mybir.AluOpType
COPY = mybir.ActivationFunctionType.Copy

P = 128
B = 8
S = 49
H = 512
R = 3
Q = (S - 1) // R
PACK = 4
HALF = 2

FLOPS = 2 * 2 * B * (S - 1) * H * H


def tile_sindylossmixin_pa_s_kernel(tc, x, k1, k2, coefficients, out):
    nc = tc.nc
    with ExitStack() as ctx:
        keep = ctx.enter_context(tc.tile_pool(name="keep", bufs=1))
        psum = ctx.enter_context(tc.psum_pool(name="psum", bufs=1))
        ctx.enter_context(tc.manual_schedule())

        x_sb = keep.tile([P, R + 1, H], BF16)
        k1_sb = keep.tile([P, R, H], BF16)
        k2_sb = keep.tile([P, R, H], BF16)
        c_sb = keep.tile([P, HALF, HALF, H], BF16)
        nc.sync.dma_start(
            out=x_sb[:, 0:R, :].rearrange("p r h -> p (r h)"),
            in_=x[:, 0 : S - 1, :].rearrange("b (q r) h -> q b (r h)", r=R),
        )
        nc.sync.dma_start(
            out=x_sb[:, R, :],
            in_=x[:, 1:S, :].rearrange("b (q r) h -> q b r h", r=R)[:, :, R - 1, :],
        )
        nc.sync.dma_start(
            out=k2_sb[:].rearrange("p r h -> p (r h)"),
            in_=k2.rearrange("(b q r) h -> q b (r h)", b=B, q=Q, r=R),
        )
        nc.sync.dma_start(
            out=k1_sb[:].rearrange("p r h -> p (r h)"),
            in_=k1.rearrange("(b q r) h -> q b (r h)", b=B, q=Q, r=R),
        )
        c_rows = coefficients.rearrange("(u m e) j -> e m u j", u=HALF, e=HALF)
        for e in range(HALF):
            nc.sync.dma_start(out=c_sb[:, e, :, :], in_=c_rows[e])

        ident = keep.tile([P, P], F32)
        make_identity(nc, ident[:])

        warm = keep.tile([P, 2], F32)
        nc.vector.memset(warm[:, 0:1], 0.0)
        nc.scalar.activation(out=warm[:, 1:2], in_=warm[:, 0:1], func=COPY)

        def transpose_words(bank, words):
            for u in range(HALF):
                nc.tensor.transpose(bank[:, u, :], words[:, u * P : (u + 1) * P], ident[:])

        x_words = x_sb[:].bitcast(F32)
        k2_words = k2_sb[:].bitcast(F32)
        c_words = c_sb[:].bitcast(F32)
        yT = keep.tile([P, R, P, PACK], BF16, align_bytes=64)
        half_k2T = keep.tile([P, R, P, PACK], BF16, align_bytes=64)
        aT = keep.tile([P, R, P, PACK], BF16, align_bytes=64)
        zT = keep.tile([P, R, P, PACK], BF16, align_bytes=64)
        cT = keep.tile([P, H, PACK], BF16, align_bytes=64)
        a_codes = keep.tile([P, R * P], U32, align_bytes=64)
        a_scales = keep.tile([P, R * P], U8, align_bytes=64)
        z_codes = keep.tile([P, R * P], U32, align_bytes=64)
        z_scales = keep.tile([P, R * P], U8, align_bytes=64)
        c_codes = keep.tile([P, H], U32, align_bytes=64)
        c_scales = keep.tile([P, H], U8, align_bytes=64)
        diff = keep.tile([P, R, H], F32)
        k_sum = keep.tile([P, R, H], F32)
        base = keep.tile([P, R, H], F32)
        result = keep.tile([P, R, H], F32)

        def quantise(codes, scales, cols, grouped):
            nc.vector.quantize_mx(
                out=codes[:, cols].bitcast(FP8X4), scales=scales[:, cols], in_=grouped
            )

        def chunk(r):
            return slice(r * P, (r + 1) * P)

        def add_k_sum(rows):
            nc.vector.scalar_tensor_tensor(
                out=k_sum[:, rows, :],
                in0=k2_sb[:, rows, :],
                scalar=2.0,
                in1=k1_sb[:, rows, :],
                op0=ALU.mult,
                op1=ALU.add,
            )

        for r in range(R):
            yT_ps = psum.tile([P, HALF, P], F32, tag="y_then_k3", bufs=R)
            transpose_words(yT_ps, x_words[:, r, :])
            nc.scalar.copy(
                out=yT[:, r, :, :].bitcast(F32), in_=yT_ps[:].rearrange("p u n -> p n u")
            )
        nc.vector.tensor_tensor(
            out=diff[:], in0=x_sb[:, 0:R, :], in1=x_sb[:, 1 : R + 1, :], op=ALU.subtract
        )

        for r in range(R):
            k2T_ps = psum.tile([P, HALF, P], F32, tag="k2_then_sum", bufs=R)
            transpose_words(k2T_ps, k2_words[:, r, :])
            nc.scalar.activation(
                out=half_k2T[:, r, :, :].rearrange("p n (u e) -> p n u e", e=HALF),
                in_=k2T_ps[:].bitcast(BF16).rearrange("p u (n e) -> p n u e", e=HALF),
                func=COPY,
                scale=0.5,
            )
        add_k_sum(slice(0, R - 1))
        nc.vector.tensor_tensor(out=aT[:], in0=yT[:], in1=half_k2T[:], op=ALU.add)

        for e in range(HALF):
            cT_ps = psum.tile([P, HALF, HALF, P], F32, tag="c", bufs=HALF)
            for u in range(HALF):
                transpose_words(cT_ps[:, u, :, :], c_words[:, e, u, :])
            cols = slice(e * HALF * P, (e + 1) * HALF * P)
            nc.scalar.copy(
                out=cT[:, cols, :].bitcast(F32).rearrange("p (u m) w -> p u m w", u=HALF),
                in_=cT_ps[:].rearrange("p u w m -> p u m w"),
            )
        half_cols = [slice(e * HALF * P, (e + 1) * HALF * P) for e in range(HALF)]
        quantise(c_codes, c_scales, half_cols[0], cT[:, half_cols[0], :].rearrange("p i t -> p (i t)"))
        quantise(a_codes, a_scales, chunk(0), aT[:, 0, :, :].rearrange("p n t -> p (n t)"))
        quantise(c_codes, c_scales, half_cols[1], cT[:, half_cols[1], :].rearrange("p i t -> p (i t)"))
        for r in range(1, R):
            quantise(a_codes, a_scales, chunk(r), aT[:, r, :, :].rearrange("p n t -> p (n t)"))
        add_k_sum(slice(R - 1, R))
        nc.vector.scalar_tensor_tensor(
            out=base[:], in0=k_sum[:], scalar=1.0 / 6.0, in1=diff[:], op0=ALU.mult, op1=ALU.add
        )

        k3T_banks = []
        for r in range(R):
            k3T_ps = psum.tile([P, PACK, P], F32, tag="y_then_k3", bufs=R)
            k3T_banks.append(k3T_ps)
            for g in range(PACK):
                nc.tensor.matmul_mx(
                    out=k3T_ps[:, g, :],
                    lhsT=c_codes[:, chunk(g)].bitcast(FP8X4),
                    lhsT_scale=c_scales[:, chunk(g)],
                    rhs=a_codes[:, chunk(r)].bitcast(FP8X4),
                    rhs_scale=a_scales[:, chunk(r)],
                    start=True,
                    stop=True,
                )

        def row_pass(bank, codes, scales, r, start, stop):
            nc.tensor.matmul_mx(
                out=bank[:],
                lhsT=codes[:, chunk(r)].bitcast(FP8X4),
                lhsT_scale=scales[:, chunk(r)],
                rhs=c_codes[:].bitcast(FP8X4),
                rhs_scale=c_scales[:],
                start=start,
                stop=stop,
            )

        sum_banks = []
        for r in range(R):
            sum_ps = psum.tile([P, H], F32, tag="k2_then_sum", bufs=R)
            sum_banks.append(sum_ps)
            row_pass(sum_ps, a_codes, a_scales, r, True, False)
            row_pass(sum_ps, a_codes, a_scales, r, False, False)

        for r in range(R + 1):
            if r < R:
                nc.vector.tensor_tensor(
                    out=zT[:, r, :, :].rearrange("p n (u e) -> p n u e", e=HALF),
                    in0=k3T_banks[r][:].rearrange("p (e u) n -> p n u e", e=HALF),
                    in1=yT[:, r, :, :].rearrange("p n (u e) -> p n u e", e=HALF),
                    op=ALU.add,
                )
            if r > 0:
                quantise(
                    z_codes, z_scales, chunk(r - 1), zT[:, r - 1, :, :].rearrange("p n t -> p (n t)")
                )

        out_rows = out.rearrange("b (q r) h -> q b r h", r=R)
        for r in range(R):
            sum_ps = sum_banks[r]
            row_pass(sum_ps, z_codes, z_scales, r, False, True)
            nc.vector.scalar_tensor_tensor(
                out=result[:, r, :].rearrange("p (c e) -> p c e", e=HALF),
                in0=sum_ps[:].rearrange("p (e c) -> p c e", e=HALF),
                scalar=1.0 / 6.0,
                in1=base[:, r, :].rearrange("p (c e) -> p c e", e=HALF),
                op0=ALU.mult,
                op1=ALU.add,
            )
            nc.sync.dma_start(out=out_rows[:, :, r, :], in_=result[:, r, :])
